import numpy as np
import ml_dtypes


def mxq(x, axis, fmt="e4m3"):
    dtype, down = {"e4m3": (ml_dtypes.float8_e4m3fn, 7), "e5m2": (ml_dtypes.float8_e5m2, 14)}[fmt]
    v = np.moveaxis(np.asarray(x, np.float32).astype(ml_dtypes.bfloat16).astype(np.float64), axis, -1)
    blocks = v.reshape(v.shape[:-1] + (-1, 32))
    amax = np.abs(blocks).max(-1, keepdims=True)
    byte = np.maximum(np.where(amax > 0, np.frexp(amax)[1] - 1 + 127, 0) - down, 1)
    scale = np.exp2(byte - 127.0)
    codes = (blocks / scale).astype(np.float32).astype(dtype).astype(np.float64)
    return np.moveaxis((codes * scale).reshape(v.shape), -1, axis)


WIDE = False


def mx_kscale(k):
    if not WIDE:
        return np.ones(k)
    levels = np.array([10, -10, 5, -5, 0])
    a = np.random.permutation(np.resize(levels, k // 512 * 4)).reshape(k // 512, 4)
    idx = np.arange(k)
    return np.exp2(a[idx // 512, idx % 128 // 32])


BF16 = ml_dtypes.bfloat16


def bf(x):
    return np.asarray(x, np.float32).astype(BF16)


def f64(x):
    return np.asarray(x).astype(np.float64)


BH, S, D = 16, 512, 256
ALPHA = 0.99
EPS = 1e-10
LOG_DECAY = np.log(ALPHA ** np.arange(S - 1.0, -1.0, -1.0) + EPS)


def setup_inputs():
    s = mx_kscale(S)
    decay = np.exp(LOG_DECAY)
    c = (decay * s).sum() / decay.sum()
    a = 1.2 / D ** 0.25
    return {"q": bf(np.random.standard_normal((BH, S, D)) * a),
            "k": bf(np.random.standard_normal((BH, S, D)) * a),
            "v": bf(np.random.standard_normal((BH, S, D)) * 2.0 * c / s[:, None]),
            "attn_mask": bf(np.random.standard_normal((BH, S, S)) * 0.5 + np.log(s))}


def reference(q, k, v, attn_mask):
    scores = f64(q) @ f64(k).transpose(0, 2, 1) + f64(attn_mask)
    scores = scores + LOG_DECAY[None, None, :]
    e = np.exp(scores - scores.max(-1, keepdims=True))
    return (mxq(e, 2, "e4m3") @ mxq(f64(v), 1, "e4m3")) / e.sum(-1, keepdims=True)

@@ -1,0 +1,203 @@
+import math
+from contextlib import ExitStack
+
+import concourse.mybir as mybir
+from concourse.masks import make_identity
+
+F32 = mybir.dt.float32
+BF16 = mybir.dt.bfloat16
+I32 = mybir.dt.int32
+U32 = mybir.dt.uint32
+U8 = mybir.dt.uint8
+FP8X4 = mybir.dt.float8_e4m3fn_x4
+ADD = mybir.AluOpType.add
+MULT = mybir.AluOpType.mult
+MAX = mybir.AluOpType.max
+EXP = mybir.ActivationFunctionType.Exp
+COPY = mybir.ActivationFunctionType.Copy
+AX_X = mybir.AxisListType.X
+
+P = 128
+BH, S, D = 16, 512, 256
+NT = S // P
+ALPHA = 0.99
+EPS = 1e-10
+LN_ALPHA = math.log(ALPHA)
+C_HI = round(LN_ALPHA * 2097152.0) / 2097152.0
+C_LO = LN_ALPHA - C_HI
+FLOPS = 2 * 2 * BH * S * S * D
+
+LD_BUFS = 4
+
+
+def tile_dotproductattention_t_kernel(tc, q, k, v, attn_mask, out):
+    nc = tc.nc
+    with ExitStack() as ctx:
+        const = ctx.enter_context(tc.tile_pool(name="const", bufs=1))
+        ld = ctx.enter_context(tc.tile_pool(name="ld", bufs=LD_BUFS))
+        tp = ctx.enter_context(tc.tile_pool(name="tp", bufs=2))
+        sc = ctx.enter_context(tc.tile_pool(name="sc", bufs=4))
+        mx = ctx.enter_context(tc.tile_pool(name="mx", bufs=3))
+        sm = ctx.enter_context(tc.tile_pool(name="sm", bufs=8))
+        ob = ctx.enter_context(tc.tile_pool(name="ob", bufs=3))
+        ps_tr = ctx.enter_context(tc.psum_pool(name="ps_tr", bufs=2))
+        ps_s = ctx.enter_context(tc.psum_pool(name="ps_s", bufs=3))
+        ps_et = ctx.enter_context(tc.psum_pool(name="ps_et", bufs=2))
+        ps_o = ctx.enter_context(tc.psum_pool(name="ps_o", bufs=1))
+
+        ident32 = const.tile([P, P], F32)
+        make_identity(nc, ident32[:])
+        identb = const.tile([P, P], BF16)
+        make_identity(nc, identb[:])
+
+        j_i = const.tile([P, NT], I32)
+        nc.gpsimd.iota(j_i[:], pattern=[[P, NT]], base=0, channel_multiplier=1)
+        j_f = const.tile([P, NT], F32)
+        nc.vector.tensor_copy(out=j_f[:], in_=j_i[:])
+        n_f = const.tile([P, NT], F32)
+        nc.vector.tensor_scalar(out=n_f[:], in0=j_f[:], scalar1=-1.0, scalar2=float(S - 1), op0=MULT, op1=ADD)
+        grow = const.tile([P, NT], F32)
+        nc.scalar.activation(out=grow[:], in_=n_f[:], func=EXP, scale=-LN_ALPHA)
+        low = const.tile([P, NT], F32)
+        nc.vector.tensor_scalar(out=low[:], in0=n_f[:], scalar1=C_LO, scalar2=None, op0=MULT)
+        low2 = const.tile([P, NT], F32)
+        nc.vector.scalar_tensor_tensor(out=low2[:], in0=grow[:], scalar=EPS, in1=low[:], op0=MULT, op1=ADD)
+        dcol = const.tile([P, NT], F32)
+        nc.vector.scalar_tensor_tensor(out=dcol[:], in0=n_f[:], scalar=C_HI, in1=low2[:], op0=MULT, op1=ADD)
+
+        heads = {}
+
+        def load(h):
+            q_sb = ld.tile([P, NT * D], BF16, tag="q", name="q_sb")
+            nc.sync.dma_start(out=q_sb[:], in_=q[h].rearrange("(p t) d -> p (t d)", t=NT))
+            k_sb = ld.tile([P, NT * D], BF16, tag="k", name="k_sb")
+            nc.sync.dma_start(out=k_sb[:], in_=k[h].rearrange("(p t) d -> p (t d)", t=NT))
+            m_sb = ld.tile([P, NT * S], BF16, tag="m", name="m_sb")
+            nc.sync.dma_start(out=m_sb[:], in_=attn_mask[h].rearrange("(p t) j -> p (t j)", t=NT))
+            v_sb = ld.tile([P, NT * D], BF16, tag="v", name="v_sb")
+            nc.sync.dma_start(
+                out=v_sb[:].rearrange("p (t d) -> p t d", t=NT),
+                in_=v[h].rearrange("(t p) d -> p t d", p=P),
+            )
+            heads[h] = {"q": q_sb, "k": k_sb, "m": m_sb, "v": v_sb}
+
+        def prep(h):
+            st = heads[h]
+            q32 = st["q"][:].bitcast(F32)
+            k32 = st["k"][:].bitcast(F32)
+            qT_ps = ps_tr.tile([P, S], F32, tag="tr", name="qT_ps")
+            for t in range(NT):
+                nc.tensor.transpose(qT_ps[:, t * P:(t + 1) * P], q32[:, t * P:(t + 1) * P], ident32[:])
+            kT_ps = ps_tr.tile([P, S], F32, tag="tr", name="kT_ps")
+            for t in range(NT):
+                nc.tensor.transpose(kT_ps[:, t * P:(t + 1) * P], k32[:, t * P:(t + 1) * P], ident32[:])
+            qT = tp.tile([P, S], F32, tag="qT", name="qT")
+            nc.scalar.copy(out=qT[:], in_=qT_ps[:])
+            kT = tp.tile([P, S], F32, tag="kT", name="kT")
+            nc.scalar.copy(
+                out=kT[:].rearrange("w (p t) -> w p t", t=NT),
+                in_=kT_ps[:].rearrange("w (t p) -> w p t", t=NT),
+            )
+            st["qTb"] = qT[:].bitcast(BF16).rearrange("w (t p e) -> w t p e", t=NT, e=2)
+            st["kTb"] = kT[:].bitcast(BF16).rearrange("w (j e) -> w j e", e=2)
+            vg = mx.tile([P, D * NT], BF16, tag="vg", name="vg", align_bytes=64)
+            nc.vector.tensor_copy(
+                out=vg[:].rearrange("p (c i t) -> p c t i", i=4, t=NT),
+                in_=st["v"][:].rearrange("p (t c i) -> p c t i", t=NT, i=4),
+            )
+            vcod = mx.tile([P, D], U32, tag="vcod", name="vcod", align_bytes=64)
+            vscl = mx.tile([P, D], U8, tag="vscl", name="vscl", align_bytes=64)
+            nc.vector.quantize_mx(out=vcod[:].bitcast(FP8X4), scales=vscl[:], in_=vg[:])
+            st["vcod"] = vcod
+            st["vscl"] = vscl
+            o_sb = ob.tile([P, NT * D], F32, tag="o_sb", name="o_sb")
+            st["o_sb"] = o_sb
+
+        def front(h, half):
+            st = heads[h]
+            rsum = sm.tile([P, 2], F32, tag="rsum", name="rsum")
+            es = []
+            for a in range(2):
+                t = 2 * half + a
+                s_ps = ps_s.tile([P, S], F32, tag="s", name="s_ps")
+                nc.tensor.matmul(s_ps[:], lhsT=st["qTb"][:, t, :, 0], rhs=st["kTb"][:, :, 0], start=True, stop=False)
+                for c in range(NT):
+                    nc.tensor.matmul(
+                        s_ps[:, c * P:(c + 1) * P],
+                        lhsT=dcol[:, c:c + 1].to_broadcast([P, P]),
+                        rhs=ident32[:],
+                        start=False,
+                        stop=False,
+                        is_transpose=True,
+                    )
+                nc.tensor.matmul(s_ps[:], lhsT=st["qTb"][:, t, :, 1], rhs=st["kTb"][:, :, 1], start=False, stop=True)
+                s_sb = sc.tile([P, S], F32, tag="s_sb", name="s_sb")
+                nc.vector.tensor_tensor(out=s_sb[:], in0=s_ps[:], in1=st["m"][:, t * S:(t + 1) * S], op=ADD)
+                negm = sm.tile([P, 1], F32, tag="negm", name="negm")
+                nc.vector.tensor_reduce(out=negm[:], in_=s_sb[:], axis=AX_X, op=MAX, negate=True)
+                e_sb = sc.tile([P, S], BF16, tag="e_sb", name="e_sb")
+                nc.scalar.activation(
+                    out=e_sb[:], in_=s_sb[:], func=EXP, bias=negm[:], scale=1.0, accum_out=rsum[:, a:a + 1]
+                )
+                es.append(e_sb)
+            st["es"] = es
+            st["rsum"] = rsum
+
+        def back(h, half, es, rsum):
+            st = heads[h]
+            eT_ps = ps_et.tile([P, 2, NT, P], BF16, tag="et", name="eT_ps")
+            for a in range(2):
+                for c in range(NT):
+                    nc.tensor.transpose(eT_ps[:, a, c, :], es[a][:, c * P:(c + 1) * P], identb[:])
+            grp = mx.tile([P, 2 * P * NT], BF16, tag="grp", name="grp", align_bytes=64)
+            nc.scalar.copy(
+                out=grp[:].rearrange("p (a i c) -> p a i c", a=2, c=NT),
+                in_=eT_ps[:].rearrange("p a c i -> p a i c"),
+            )
+            ecod = mx.tile([P, 2 * P], U32, tag="ecod", name="ecod", align_bytes=64)
+            escl = mx.tile([P, 2 * P], U8, tag="escl", name="escl", align_bytes=64)
+            nc.vector.quantize_mx(out=ecod[:].bitcast(FP8X4), scales=escl[:], in_=grp[:])
+            rinv = sm.tile([P, 2], F32, tag="rinv", name="rinv")
+            nc.vector.reciprocal(rinv[:], rsum[:])
+            o_ps = ps_o.tile([P, 2, D], F32, tag="o", name="o_ps")
+            for a in range(2):
+                nc.tensor.matmul_mx(
+                    out=o_ps[:, a, :],
+                    lhsT=ecod[:, a * P:(a + 1) * P].bitcast(FP8X4),
+                    lhsT_scale=escl[:, a * P:(a + 1) * P],
+                    rhs=st["vcod"][:].bitcast(FP8X4),
+                    rhs_scale=st["vscl"][:],
+                    start=True,
+                    stop=True,
+                )
+            for a in range(2):
+                t = 2 * half + a
+                if half == 1 and a == 1:
+                    nc.vector.tensor_scalar(
+                        out=st["o_sb"][:, t * D:(t + 1) * D], in0=o_ps[:, a, :], scalar1=rinv[:, a:a + 1],
+                        scalar2=None, op0=MULT,
+                    )
+                else:
+                    nc.scalar.activation(
+                        out=st["o_sb"][:, t * D:(t + 1) * D], in_=o_ps[:, a, :], func=COPY, scale=rinv[:, a:a + 1]
+                    )
+            if half == 1:
+                nc.gpsimd.dma_start(out=out[h].rearrange("(p t) d -> p (t d)", t=NT), in_=st["o_sb"][:])
+
+        for h in range(min(LD_BUFS - 1, BH)):
+            load(h)
+        prep(0)
+        pending = []
+        for h in range(BH):
+            for half in range(2):
+                front(h, half)
+                pending.append((h, half, heads[h]["es"], heads[h]["rsum"]))
+                if half == 0:
+                    if h + LD_BUFS - 1 < BH:
+                        load(h + LD_BUFS - 1)
+                    if h + 1 < BH:
+                        prep(h + 1)
+                if len(pending) > 1:
+                    back(*pending.pop(0))
+        while pending:
+            back(*pending.pop(0))

@@ -20,6 +20,8 @@ AX_X = mybir.AxisListType.X
 P = 128
 BH, S, D = 16, 512, 256
 NT = S // P
+NTILES = BH * NT
+NPAIRS = NTILES // 2
 ALPHA = 0.99
 EPS = 1e-10
 LN_ALPHA = math.log(ALPHA)
@@ -27,23 +29,25 @@ C_HI = round(LN_ALPHA * 2097152.0) / 2097152.0
 C_LO = LN_ALPHA - C_HI
 FLOPS = 2 * 2 * BH * S * S * D
 
-LD_BUFS = 4
+LA = 3
+XMODE = "g"
+PIN = True
+PEMASK = ()
+TAILS = 0
 
 
 def tile_dotproductattention_t_kernel(tc, q, k, v, attn_mask, out):
     nc = tc.nc
     with ExitStack() as ctx:
         const = ctx.enter_context(tc.tile_pool(name="const", bufs=1))
-        ld = ctx.enter_context(tc.tile_pool(name="ld", bufs=LD_BUFS))
-        tp = ctx.enter_context(tc.tile_pool(name="tp", bufs=2))
-        sc = ctx.enter_context(tc.tile_pool(name="sc", bufs=4))
-        mx = ctx.enter_context(tc.tile_pool(name="mx", bufs=3))
-        sm = ctx.enter_context(tc.tile_pool(name="sm", bufs=8))
-        ob = ctx.enter_context(tc.tile_pool(name="ob", bufs=3))
-        ps_tr = ctx.enter_context(tc.psum_pool(name="ps_tr", bufs=2))
+        ld = ctx.enter_context(tc.tile_pool(name="ld", bufs=LA + 1))
+        wk = ctx.enter_context(tc.tile_pool(name="wk", bufs=2))
+        ps_tr = ctx.enter_context(tc.psum_pool(name="ps_tr", bufs=1))
         ps_s = ctx.enter_context(tc.psum_pool(name="ps_s", bufs=3))
         ps_et = ctx.enter_context(tc.psum_pool(name="ps_et", bufs=2))
-        ps_o = ctx.enter_context(tc.psum_pool(name="ps_o", bufs=1))
+        ps_o = ctx.enter_context(tc.psum_pool(name="ps_o", bufs=2))
+        if PIN:
+            ctx.enter_context(tc.manual_schedule())
 
         ident32 = const.tile([P, P], F32)
         make_identity(nc, ident32[:])
@@ -65,9 +69,13 @@ def tile_dotproductattention_t_kernel(tc, q, k, v, attn_mask, out):
         dcol = const.tile([P, NT], F32)
         nc.vector.scalar_tensor_tensor(out=dcol[:], in0=n_f[:], scalar=C_HI, in1=low2[:], op0=MULT, op1=ADD)
 
-        heads = {}
+        hd = {}
+        pr = {}
+        tl = {}
 
         def load(h):
+            if h < 0 or h >= BH:
+                return
             q_sb = ld.tile([P, NT * D], BF16, tag="q", name="q_sb")
             nc.sync.dma_start(out=q_sb[:], in_=q[h].rearrange("(p t) d -> p (t d)", t=NT))
             k_sb = ld.tile([P, NT * D], BF16, tag="k", name="k_sb")
@@ -79,125 +87,232 @@ def tile_dotproductattention_t_kernel(tc, q, k, v, attn_mask, out):
                 out=v_sb[:].rearrange("p (t d) -> p t d", t=NT),
                 in_=v[h].rearrange("(t p) d -> p t d", p=P),
             )
-            heads[h] = {"q": q_sb, "k": k_sb, "m": m_sb, "v": v_sb}
+            hd[h] = {"q": q_sb, "k": k_sb, "m": m_sb, "v": v_sb}
 
-        def prep(h):
-            st = heads[h]
-            q32 = st["q"][:].bitcast(F32)
-            k32 = st["k"][:].bitcast(F32)
-            qT_ps = ps_tr.tile([P, S], F32, tag="tr", name="qT_ps")
+        def tqk(h, which):
+            if h < 0 or h >= BH:
+                return
+            src = hd[h][which][:].bitcast(F32)
+            t_ps = ps_tr.tile([P, S], F32, tag="tr", name="t_ps")
             for t in range(NT):
-                nc.tensor.transpose(qT_ps[:, t * P:(t + 1) * P], q32[:, t * P:(t + 1) * P], ident32[:])
-            kT_ps = ps_tr.tile([P, S], F32, tag="tr", name="kT_ps")
-            for t in range(NT):
-                nc.tensor.transpose(kT_ps[:, t * P:(t + 1) * P], k32[:, t * P:(t + 1) * P], ident32[:])
-            qT = tp.tile([P, S], F32, tag="qT", name="qT")
-            nc.scalar.copy(out=qT[:], in_=qT_ps[:])
-            kT = tp.tile([P, S], F32, tag="kT", name="kT")
+                nc.tensor.transpose(t_ps[:, t * P:(t + 1) * P], src[:, t * P:(t + 1) * P], ident32[:])
+            hd[h][which + "ps"] = t_ps
+
+        def xq(h):
+            if h < 0 or h >= BH:
+                return
+            qT = wk.tile([P, S], F32, tag="qT", name="qT", bufs=2)
+            nc.scalar.copy(out=qT[:], in_=hd[h]["qps"][:])
+            hd[h]["qTb"] = qT[:].bitcast(BF16).rearrange("w (t p e) -> w t p e", t=NT, e=2)
+
+        def xk(h):
+            if h < 0 or h >= BH:
+                return
+            kT = wk.tile([P, S], F32, tag="kT", name="kT", bufs=2)
             nc.scalar.copy(
                 out=kT[:].rearrange("w (p t) -> w p t", t=NT),
-                in_=kT_ps[:].rearrange("w (t p) -> w p t", t=NT),
+                in_=hd[h]["kps"][:].rearrange("w (t p) -> w p t", t=NT),
             )
-            st["qTb"] = qT[:].bitcast(BF16).rearrange("w (t p e) -> w t p e", t=NT, e=2)
-            st["kTb"] = kT[:].bitcast(BF16).rearrange("w (j e) -> w j e", e=2)
-            vg = mx.tile([P, D * NT], BF16, tag="vg", name="vg", align_bytes=64)
+            hd[h]["kTb"] = kT[:].bitcast(BF16).rearrange("w (j e) -> w j e", e=2)
+
+        def rgv(h):
+            if h < 0 or h >= BH:
+                return
+            vg = wk.tile([P, D * NT], BF16, tag="vg", name="vg", align_bytes=64, bufs=2)
             nc.vector.tensor_copy(
                 out=vg[:].rearrange("p (c i t) -> p c t i", i=4, t=NT),
-                in_=st["v"][:].rearrange("p (t c i) -> p c t i", t=NT, i=4),
+                in_=hd[h]["v"][:].rearrange("p (t c i) -> p c t i", t=NT, i=4),
             )
-            vcod = mx.tile([P, D], U32, tag="vcod", name="vcod", align_bytes=64)
-            vscl = mx.tile([P, D], U8, tag="vscl", name="vscl", align_bytes=64)
-            nc.vector.quantize_mx(out=vcod[:].bitcast(FP8X4), scales=vscl[:], in_=vg[:])
-            st["vcod"] = vcod
-            st["vscl"] = vscl
-            o_sb = ob.tile([P, NT * D], F32, tag="o_sb", name="o_sb")
-            st["o_sb"] = o_sb
+            hd[h]["vg"] = vg
 
-        def front(h, half):
-            st = heads[h]
-            rsum = sm.tile([P, 2], F32, tag="rsum", name="rsum")
-            es = []
-            for a in range(2):
-                t = 2 * half + a
+        def qv(h):
+            if h < 0 or h >= BH:
+                return
+            vcod = wk.tile([P, D], U32, tag="vcod", name="vcod", align_bytes=64, bufs=3)
+            vscl = wk.tile([P, D], U8, tag="vscl", name="vscl", align_bytes=64, bufs=3)
+            nc.vector.quantize_mx(out=vcod[:].bitcast(FP8X4), scales=vscl[:], in_=hd[h]["vg"][:])
+            hd[h]["vcod"] = vcod
+            hd[h]["vscl"] = vscl
+
+        def qk_et(kq, ke):
+            do_q = 0 <= kq < NTILES
+            do_e = 0 <= ke < NTILES
+            if do_q:
+                st = hd[kq // NT]
+                t = kq % NT
                 s_ps = ps_s.tile([P, S], F32, tag="s", name="s_ps")
-                nc.tensor.matmul(s_ps[:], lhsT=st["qTb"][:, t, :, 0], rhs=st["kTb"][:, :, 0], start=True, stop=False)
-                for c in range(NT):
-                    nc.tensor.matmul(
-                        s_ps[:, c * P:(c + 1) * P],
-                        lhsT=dcol[:, c:c + 1].to_broadcast([P, P]),
-                        rhs=ident32[:],
-                        start=False,
-                        stop=False,
-                        is_transpose=True,
-                    )
-                nc.tensor.matmul(s_ps[:], lhsT=st["qTb"][:, t, :, 1], rhs=st["kTb"][:, :, 1], start=False, stop=True)
-                s_sb = sc.tile([P, S], F32, tag="s_sb", name="s_sb")
-                nc.vector.tensor_tensor(out=s_sb[:], in0=s_ps[:], in1=st["m"][:, t * S:(t + 1) * S], op=ADD)
-                negm = sm.tile([P, 1], F32, tag="negm", name="negm")
-                nc.vector.tensor_reduce(out=negm[:], in_=s_sb[:], axis=AX_X, op=MAX, negate=True)
-                e_sb = sc.tile([P, S], BF16, tag="e_sb", name="e_sb")
-                nc.scalar.activation(
-                    out=e_sb[:], in_=s_sb[:], func=EXP, bias=negm[:], scale=1.0, accum_out=rsum[:, a:a + 1]
-                )
-                es.append(e_sb)
-            st["es"] = es
-            st["rsum"] = rsum
+                tl[kq] = {"s_ps": s_ps}
+            if do_e:
+                n = ke // 2
+                a = ke % 2
+                if a == 0:
+                    eT_new = ps_et.tile([P, 2, NT, P], BF16, tag="et", name="eT_ps")
+                    pr[n]["eT_ps"] = eT_new
+                eT_ps = pr[n]["eT_ps"]
+                e_sb = tl[ke]["e_sb"]
 
-        def back(h, half, es, rsum):
-            st = heads[h]
-            eT_ps = ps_et.tile([P, 2, NT, P], BF16, tag="et", name="eT_ps")
-            for a in range(2):
-                for c in range(NT):
-                    nc.tensor.transpose(eT_ps[:, a, c, :], es[a][:, c * P:(c + 1) * P], identb[:])
-            grp = mx.tile([P, 2 * P * NT], BF16, tag="grp", name="grp", align_bytes=64)
-            nc.scalar.copy(
-                out=grp[:].rearrange("p (a i c) -> p a i c", a=2, c=NT),
-                in_=eT_ps[:].rearrange("p a c i -> p a i c"),
+            def dec(c, last):
+                nc.tensor.matmul(
+                    s_ps[:, c * P:(c + 1) * P],
+                    lhsT=dcol[:, c:c + 1].to_broadcast([P, P]),
+                    rhs=ident32[:],
+                    start=False,
+                    stop=last,
+                    is_transpose=True,
+                )
+
+            def etr(c):
+                nc.tensor.transpose(eT_ps[:, a, c, :], e_sb[:, c * P:(c + 1) * P], identb[:])
+
+            if do_q:
+                nc.tensor.matmul(s_ps[:], lhsT=st["qTb"][:, t, :, 0], rhs=st["kTb"][:, :, 0], start=True, stop=False)
+                if kq in PEMASK:
+                    nc.tensor.matmul(s_ps[:], lhsT=identb[:], rhs=st["m"][:, t * S:(t + 1) * S], start=False, stop=False)
+                dec(0, False)
+                dec(1, False)
+            if do_e:
+                etr(0)
+                etr(1)
+            if do_q:
+                nc.tensor.matmul(s_ps[:], lhsT=st["qTb"][:, t, :, 1], rhs=st["kTb"][:, :, 1], start=False, stop=False)
+                dec(2, False)
+                dec(3, True)
+            if do_e:
+                etr(2)
+                etr(3)
+
+        def bc(kk):
+            if kk < 0 or kk >= NTILES:
+                return
+            st = hd[kk // NT]
+            t = kk % NT
+            negm = wk.tile([P, 1], F32, tag="negm", name="negm", bufs=4)
+            if kk in PEMASK:
+                nc.vector.tensor_reduce(out=negm[:], in_=tl[kk]["s_ps"][:], axis=AX_X, op=MAX, negate=True)
+                tl[kk]["s_src"] = tl[kk]["s_ps"]
+            else:
+                s_sb = wk.tile([P, S], F32, tag="s_sb", name="s_sb", bufs=4)
+                nc.vector.tensor_tensor(out=s_sb[:], in0=tl[kk]["s_ps"][:], in1=st["m"][:, t * S:(t + 1) * S], op=ADD)
+                nc.vector.tensor_reduce(out=negm[:], in_=s_sb[:], axis=AX_X, op=MAX, negate=True)
+                tl[kk]["s_src"] = s_sb
+            tl[kk]["negm"] = negm
+
+        def dexp(kk):
+            if kk < 0 or kk >= NTILES:
+                return
+            n = kk // 2
+            a = kk % 2
+            if a == 0:
+                rsum_new = wk.tile([P, 2], F32, tag="rsum", name="rsum", bufs=6)
+                pr[n] = {"rsum": rsum_new}
+            e_sb = wk.tile([P, S], BF16, tag="e_sb", name="e_sb", bufs=4)
+            nc.scalar.activation(
+                out=e_sb[:], in_=tl[kk]["s_src"][:], func=EXP, bias=tl[kk]["negm"][:], scale=1.0,
+                accum_out=pr[n]["rsum"][:, a:a + 1],
             )
-            ecod = mx.tile([P, 2 * P], U32, tag="ecod", name="ecod", align_bytes=64)
-            escl = mx.tile([P, 2 * P], U8, tag="escl", name="escl", align_bytes=64)
-            nc.vector.quantize_mx(out=ecod[:].bitcast(FP8X4), scales=escl[:], in_=grp[:])
-            rinv = sm.tile([P, 2], F32, tag="rinv", name="rinv")
-            nc.vector.reciprocal(rinv[:], rsum[:])
+            tl[kk]["e_sb"] = e_sb
+
+        def xe(n):
+            if n < 0 or n >= NPAIRS:
+                return
+            grp = wk.tile([P, 2 * P * NT], BF16, tag="grp", name="grp", align_bytes=64, bufs=3)
+            if XMODE == "g" and n < NPAIRS - TAILS:
+                etc = wk.tile([P, 2 * NT * P], BF16, tag="etc", name="etc", bufs=3)
+                nc.scalar.copy(out=etc[:], in_=pr[n]["eT_ps"][:].rearrange("p a c i -> p (a c i)"))
+                nc.gpsimd.tensor_scalar(
+                    out=grp[:].rearrange("p (a i c) -> p a i c", a=2, c=NT),
+                    in0=etc[:].rearrange("p (a c i) -> p a i c", a=2, c=NT),
+                    scalar1=1.0, scalar2=0.0, op0=MULT, op1=ADD,
+                )
+            else:
+                nc.scalar.copy(
+                    out=grp[:].rearrange("p (a i c) -> p a i c", a=2, c=NT),
+                    in_=pr[n]["eT_ps"][:].rearrange("p a c i -> p a i c"),
+                )
+            pr[n]["grp"] = grp
+
+        def qe(n):
+            if n < 0 or n >= NPAIRS:
+                return
+            ecod = wk.tile([P, 2 * P], U32, tag="ecod", name="ecod", align_bytes=64, bufs=3)
+            escl = wk.tile([P, 2 * P], U8, tag="escl", name="escl", align_bytes=64, bufs=3)
+            nc.vector.quantize_mx(out=ecod[:].bitcast(FP8X4), scales=escl[:], in_=pr[n]["grp"][:])
+            rinv = wk.tile([P, 2], F32, tag="rinv", name="rinv", bufs=4)
+            nc.vector.reciprocal(rinv[:], pr[n]["rsum"][:])
+            pr[n]["ecod"] = ecod
+            pr[n]["escl"] = escl
+            pr[n]["rinv"] = rinv
+
+        def pv(n):
+            if n < 0 or n >= NPAIRS:
+                return
+            st = hd[n // 2]
             o_ps = ps_o.tile([P, 2, D], F32, tag="o", name="o_ps")
             for a in range(2):
                 nc.tensor.matmul_mx(
                     out=o_ps[:, a, :],
-                    lhsT=ecod[:, a * P:(a + 1) * P].bitcast(FP8X4),
-                    lhsT_scale=escl[:, a * P:(a + 1) * P],
+                    lhsT=pr[n]["ecod"][:, a * P:(a + 1) * P].bitcast(FP8X4),
+                    lhsT_scale=pr[n]["escl"][:, a * P:(a + 1) * P],
                     rhs=st["vcod"][:].bitcast(FP8X4),
                     rhs_scale=st["vscl"][:],
                     start=True,
                     stop=True,
                 )
-            for a in range(2):
-                t = 2 * half + a
-                if half == 1 and a == 1:
-                    nc.vector.tensor_scalar(
-                        out=st["o_sb"][:, t * D:(t + 1) * D], in0=o_ps[:, a, :], scalar1=rinv[:, a:a + 1],
-                        scalar2=None, op0=MULT,
-                    )
-                else:
-                    nc.scalar.activation(
-                        out=st["o_sb"][:, t * D:(t + 1) * D], in_=o_ps[:, a, :], func=COPY, scale=rinv[:, a:a + 1]
-                    )
-            if half == 1:
-                nc.gpsimd.dma_start(out=out[h].rearrange("(p t) d -> p (t d)", t=NT), in_=st["o_sb"][:])
+            pr[n]["o_ps"] = o_ps
 
-        for h in range(min(LD_BUFS - 1, BH)):
+        def oex(kk):
+            if kk < 0 or kk >= NTILES:
+                return
+            h = kk // NT
+            t = kk % NT
+            n = kk // 2
+            a = kk % 2
+            if t == 0:
+                o_new = wk.tile([P, NT * D], F32, tag="o_sb", name="o_sb", bufs=3)
+                hd[h]["o_sb"] = o_new
+            o_sb = hd[h]["o_sb"]
+            if False:
+                nc.vector.tensor_scalar(
+                    out=o_sb[:, t * D:(t + 1) * D], in0=pr[n]["o_ps"][:, a, :], scalar1=pr[n]["rinv"][:, a:a + 1],
+                    scalar2=None, op0=MULT,
+                )
+            else:
+                nc.scalar.activation(
+                    out=o_sb[:, t * D:(t + 1) * D], in_=pr[n]["o_ps"][:, a, :], func=COPY,
+                    scale=pr[n]["rinv"][:, a:a + 1],
+                )
+
+        def store(h):
+            if h < 0 or h >= BH:
+                return
+            nc.sync.dma_start(out=out[h].rearrange("(p t) d -> p (t d)", t=NT), in_=hd[h]["o_sb"][:])
+
+        for h in range(LA):
             load(h)
-        prep(0)
-        pending = []
-        for h in range(BH):
-            for half in range(2):
-                front(h, half)
-                pending.append((h, half, heads[h]["es"], heads[h]["rsum"]))
-                if half == 0:
-                    if h + LD_BUFS - 1 < BH:
-                        load(h + LD_BUFS - 1)
-                    if h + 1 < BH:
-                        prep(h + 1)
-                if len(pending) > 1:
-                    back(*pending.pop(0))
-        while pending:
-            back(*pending.pop(0))
+        for s in range(-8, NTILES + 13):
+            if s >= 0 and s % 4 == 0:
+                load(s // 4 + LA)
+            if (s - 12) % 4 == 0:
+                store((s - 12) // 4)
+            qk_et(s + 2, s - 2)
+            if (s + 8) % 4 == 0:
+                tqk((s + 8) // 4, "q")
+            if (s + 6) % 4 == 0:
+                tqk((s + 6) // 4, "k")
+            if (s - 7) % 2 == 0:
+                pv((s - 7) // 2)
+            bc(s)
+            if (s - 6) % 2 == 0:
+                qe((s - 6) // 2)
+            if (s - 1) % 4 == 0:
+                rgv((s - 1) // 4)
+            if (s - 3) % 4 == 0:
+                qv((s - 3) // 4)
+            oex(s - 8)
+            dexp(s - 1)
+            if (s - 4) % 2 == 0:
+                xe((s - 4) // 2)
+            if (s + 7) % 4 == 0:
+                xq((s + 7) // 4)
+            if (s + 5) % 4 == 0:
+                xk((s + 5) // 4)

@@ -134,67 +134,61 @@ def tile_dotproductattention_t_kernel(tc, q, k, v, attn_mask, out):
             hd[h]["vcod"] = vcod
             hd[h]["vscl"] = vscl
 
-        def qk_et(kq, ke):
-            do_q = 0 <= kq < NTILES
-            do_e = 0 <= ke < NTILES
-            if do_q:
-                st = hd[kq // NT]
-                t = kq % NT
-                s_ps = ps_s.tile([P, S], F32, tag="s", name="s_ps")
-                tl[kq] = {"s_ps": s_ps}
-            if do_e:
-                n = ke // 2
-                a = ke % 2
-                if a == 0:
-                    eT_new = ps_et.tile([P, 2, NT, P], BF16, tag="et", name="eT_ps")
-                    pr[n]["eT_ps"] = eT_new
-                eT_ps = pr[n]["eT_ps"]
-                e_sb = tl[ke]["e_sb"]
+        def mm(kq, e):
+            if kq < 0 or kq >= NTILES:
+                return
+            st = hd[kq // NT]
+            t = kq % NT
+            if e == 0:
+                s_new = ps_s.tile([P, S], F32, tag="s", name="s_ps")
+                tl[kq] = {"s_ps": s_new}
+            s_ps = tl[kq]["s_ps"]
+            nc.tensor.matmul(s_ps[:], lhsT=st["qTb"][:, t, :, e], rhs=st["kTb"][:, :, e], start=(e == 0), stop=False)
+            if e == 1 and kq in PEMASK:
+                nc.tensor.matmul(s_ps[:], lhsT=identb[:], rhs=st["m"][:, t * S:(t + 1) * S], start=False, stop=False)
 
-            def dec(c, last):
+        def dec(kq, cs):
+            if kq < 0 or kq >= NTILES:
+                return
+            s_ps = tl[kq]["s_ps"]
+            for c in cs:
                 nc.tensor.matmul(
                     s_ps[:, c * P:(c + 1) * P],
                     lhsT=dcol[:, c:c + 1].to_broadcast([P, P]),
                     rhs=ident32[:],
                     start=False,
-                    stop=last,
+                    stop=(c == NT - 1),
                     is_transpose=True,
                 )
 
-            def etr(c):
-                nc.tensor.transpose(eT_ps[:, a, c, :], e_sb[:, c * P:(c + 1) * P], identb[:])
+        def etr(ke, cs):
+            if ke < 0 or ke >= NTILES:
+                return
+            n = ke // 2
+            a = ke % 2
+            if a == 0 and cs[0] == 0:
+                eT_new = ps_et.tile([P, 2, NT, P], BF16, tag="et", name="eT_ps")
+                pr[n]["eT_ps"] = eT_new
+            for c in cs:
+                nc.tensor.transpose(pr[n]["eT_ps"][:, a, c, :], tl[ke]["e_sb"][:, c * P:(c + 1) * P], identb[:])
 
-            if do_q:
-                nc.tensor.matmul(s_ps[:], lhsT=st["qTb"][:, t, :, 0], rhs=st["kTb"][:, :, 0], start=True, stop=False)
-                if kq in PEMASK:
-                    nc.tensor.matmul(s_ps[:], lhsT=identb[:], rhs=st["m"][:, t * S:(t + 1) * S], start=False, stop=False)
-                dec(0, False)
-                dec(1, False)
-            if do_e:
-                etr(0)
-                etr(1)
-            if do_q:
-                nc.tensor.matmul(s_ps[:], lhsT=st["qTb"][:, t, :, 1], rhs=st["kTb"][:, :, 1], start=False, stop=False)
-                dec(2, False)
-                dec(3, True)
-            if do_e:
-                etr(2)
-                etr(3)
-
-        def bc(kk):
+        def badd(kk):
             if kk < 0 or kk >= NTILES:
                 return
             st = hd[kk // NT]
             t = kk % NT
-            negm = wk.tile([P, 1], F32, tag="negm", name="negm", bufs=4)
             if kk in PEMASK:
-                nc.vector.tensor_reduce(out=negm[:], in_=tl[kk]["s_ps"][:], axis=AX_X, op=MAX, negate=True)
                 tl[kk]["s_src"] = tl[kk]["s_ps"]
             else:
-                s_sb = wk.tile([P, S], F32, tag="s_sb", name="s_sb", bufs=4)
+                s_sb = wk.tile([P, S], F32, tag="s_sb", name="s_sb", bufs=5)
                 nc.vector.tensor_tensor(out=s_sb[:], in0=tl[kk]["s_ps"][:], in1=st["m"][:, t * S:(t + 1) * S], op=ADD)
-                nc.vector.tensor_reduce(out=negm[:], in_=s_sb[:], axis=AX_X, op=MAX, negate=True)
                 tl[kk]["s_src"] = s_sb
+
+        def cmax(kk):
+            if kk < 0 or kk >= NTILES:
+                return
+            negm = wk.tile([P, 1], F32, tag="negm", name="negm", bufs=4)
+            nc.vector.tensor_reduce(out=negm[:], in_=tl[kk]["s_src"][:], axis=AX_X, op=MAX, negate=True)
             tl[kk]["negm"] = negm
 
         def dexp(kk):
@@ -294,14 +288,20 @@ def tile_dotproductattention_t_kernel(tc, q, k, v, attn_mask, out):
                 load(s // 4 + LA)
             if (s - 12) % 4 == 0:
                 store((s - 12) // 4)
-            qk_et(s + 2, s - 2)
+            mm(s + 3, 0)
+            dec(s + 2, (0, 1))
+            etr(s - 2, (0, 1))
+            mm(s + 3, 1)
+            dec(s + 2, (2, 3))
+            etr(s - 2, (2, 3))
             if (s + 8) % 4 == 0:
                 tqk((s + 8) // 4, "q")
             if (s + 6) % 4 == 0:
                 tqk((s + 6) // 4, "k")
             if (s - 7) % 2 == 0:
                 pv((s - 7) // 2)
-            bc(s)
+            badd(s + 1)
+            cmax(s)
             if (s - 6) % 2 == 0:
                 qe((s - 6) // 2)
             if (s - 1) % 4 == 0:

@@ -32,8 +32,8 @@ FLOPS = 2 * 2 * BH * S * S * D
 LA = 3
 XMODE = "g"
 PIN = True
-PEMASK = ()
-TAILS = 0
+PEMASK = tuple(range(2, 62, 5))
+TAILS = 1
 
 
 def tile_dotproductattention_t_kernel(tc, q, k, v, attn_mask, out):
@@ -43,9 +43,9 @@ def tile_dotproductattention_t_kernel(tc, q, k, v, attn_mask, out):
         ld = ctx.enter_context(tc.tile_pool(name="ld", bufs=LA + 1))
         wk = ctx.enter_context(tc.tile_pool(name="wk", bufs=2))
         ps_tr = ctx.enter_context(tc.psum_pool(name="ps_tr", bufs=1))
-        ps_s = ctx.enter_context(tc.psum_pool(name="ps_s", bufs=3))
+        ps_s = ctx.enter_context(tc.psum_pool(name="ps_s", bufs=4))
         ps_et = ctx.enter_context(tc.psum_pool(name="ps_et", bufs=2))
-        ps_o = ctx.enter_context(tc.psum_pool(name="ps_o", bufs=2))
+        ps_o = ctx.enter_context(tc.psum_pool(name="ps_o", bufs=1))
         if PIN:
             ctx.enter_context(tc.manual_schedule())
 
@@ -93,7 +93,10 @@ def tile_dotproductattention_t_kernel(tc, q, k, v, attn_mask, out):
             if h < 0 or h >= BH:
                 return
             src = hd[h][which][:].bitcast(F32)
-            t_ps = ps_tr.tile([P, S], F32, tag="tr", name="t_ps")
+            if h == 0 and which == "k":
+                t_ps = ps_o.tile([P, S], F32, tag="o", name="t_ps0")
+            else:
+                t_ps = ps_tr.tile([P, S], F32, tag="tr", name="t_ps")
             for t in range(NT):
                 nc.tensor.transpose(t_ps[:, t * P:(t + 1) * P], src[:, t * P:(t + 1) * P], ident32[:])
             hd[h][which + "ps"] = t_ps
@@ -109,10 +112,16 @@ def tile_dotproductattention_t_kernel(tc, q, k, v, attn_mask, out):
             if h < 0 or h >= BH:
                 return
             kT = wk.tile([P, S], F32, tag="kT", name="kT", bufs=2)
-            nc.scalar.copy(
-                out=kT[:].rearrange("w (p t) -> w p t", t=NT),
-                in_=hd[h]["kps"][:].rearrange("w (t p) -> w p t", t=NT),
-            )
+            if h == 0:
+                nc.vector.tensor_copy(
+                    out=kT[:].rearrange("w (p t) -> w p t", t=NT),
+                    in_=hd[h]["kps"][:].rearrange("w (t p) -> w p t", t=NT),
+                )
+            else:
+                nc.scalar.copy(
+                    out=kT[:].rearrange("w (p t) -> w p t", t=NT),
+                    in_=hd[h]["kps"][:].rearrange("w (t p) -> w p t", t=NT),
+                )
             hd[h]["kTb"] = kT[:].bitcast(BF16).rearrange("w (j e) -> w j e", e=2)
 
         def rgv(h):
@@ -196,7 +205,7 @@ def tile_dotproductattention_t_kernel(tc, q, k, v, attn_mask, out):
                 return
             n = kk // 2
             a = kk % 2
-            if a == 0:
+            if n not in pr:
                 rsum_new = wk.tile([P, 2], F32, tag="rsum", name="rsum", bufs=6)
                 pr[n] = {"rsum": rsum_new}
             e_sb = wk.tile([P, S], BF16, tag="e_sb", name="e_sb", bufs=4)
@@ -209,7 +218,7 @@ def tile_dotproductattention_t_kernel(tc, q, k, v, attn_mask, out):
         def xe(n):
             if n < 0 or n >= NPAIRS:
                 return
-            grp = wk.tile([P, 2 * P * NT], BF16, tag="grp", name="grp", align_bytes=64, bufs=3)
+            grp = wk.tile([P, 2 * P * NT], BF16, tag="grp", name="grp", align_bytes=64, bufs=1)
             if XMODE == "g" and n < NPAIRS - TAILS:
                 etc = wk.tile([P, 2 * NT * P], BF16, tag="etc", name="etc", bufs=3)
                 nc.scalar.copy(out=etc[:], in_=pr[n]["eT_ps"][:].rearrange("p a c i -> p (a c i)"))
@@ -265,7 +274,7 @@ def tile_dotproductattention_t_kernel(tc, q, k, v, attn_mask, out):
                 o_new = wk.tile([P, NT * D], F32, tag="o_sb", name="o_sb", bufs=3)
                 hd[h]["o_sb"] = o_new
             o_sb = hd[h]["o_sb"]
-            if False:
+            if n % 4 == 3:
                 nc.vector.tensor_scalar(
                     out=o_sb[:, t * D:(t + 1) * D], in0=pr[n]["o_ps"][:, a, :], scalar1=pr[n]["rinv"][:, a:a + 1],
                     scalar2=None, op0=MULT,
@@ -281,13 +290,23 @@ def tile_dotproductattention_t_kernel(tc, q, k, v, attn_mask, out):
                 return
             nc.sync.dma_start(out=out[h].rearrange("(p t) d -> p (t d)", t=NT), in_=hd[h]["o_sb"][:])
 
+        def store_half(h, half):
+            nc.sync.dma_start(
+                out=out[h].rearrange("(p t) d -> p (t d)", t=NT)[:, half * 2 * D:(half + 1) * 2 * D],
+                in_=hd[h]["o_sb"][:, half * 2 * D:(half + 1) * 2 * D],
+            )
+
         for h in range(LA):
             load(h)
         for s in range(-8, NTILES + 13):
             if s >= 0 and s % 4 == 0:
                 load(s // 4 + LA)
-            if (s - 12) % 4 == 0:
-                store((s - 12) // 4)
+            if (s - 11) % 4 == 0 and (s - 11) // 4 < BH - 1:
+                store((s - 11) // 4)
+            if s == NTILES + 5:
+                store_half(BH - 1, 0)
+            if s == NTILES + 7:
+                store_half(BH - 1, 1)
             mm(s + 3, 0)
             dec(s + 2, (0, 1))
             etr(s - 2, (0, 1))
@@ -296,23 +315,37 @@ def tile_dotproductattention_t_kernel(tc, q, k, v, attn_mask, out):
             etr(s - 2, (2, 3))
             if (s + 8) % 4 == 0:
                 tqk((s + 8) // 4, "q")
-            if (s + 6) % 4 == 0:
+            if s == -8:
+                tqk(0, "k")
+            if (s + 6) % 4 == 0 and s > -6:
                 tqk((s + 6) // 4, "k")
             if (s - 7) % 2 == 0:
                 pv((s - 7) // 2)
-            badd(s + 1)
-            cmax(s)
+            if s == -7:
+                xk(0)
+            if s + 1 in PEMASK:
+                badd(s + 1)
+                cmax(s + 1)
+            else:
+                badd(s + 1)
+            if s not in PEMASK:
+                cmax(s)
+            if (s - 2) % 4 == 0:
+                rgv((s - 2) // 4)
+            if (s - 4) % 4 == 0:
+                qv((s - 4) // 4)
             if (s - 6) % 2 == 0:
                 qe((s - 6) // 2)
-            if (s - 1) % 4 == 0:
-                rgv((s - 1) // 4)
-            if (s - 3) % 4 == 0:
-                qv((s - 3) // 4)
-            oex(s - 8)
-            dexp(s - 1)
+            if s in PEMASK:
+                dexp(s)
+            if s - 1 not in PEMASK:
+                dexp(s - 1)
             if (s - 4) % 2 == 0:
                 xe((s - 4) // 2)
+            if (s - 8) % 2 == 0:
+                oex(s - 8)
+                oex(s - 7)
             if (s + 7) % 4 == 0:
                 xq((s + 7) // 4)
-            if (s + 5) % 4 == 0:
+            if (s + 5) % 4 == 0 and s > -5:
                 xk((s + 5) // 4)

@@ -29,7 +29,7 @@ C_HI = round(LN_ALPHA * 2097152.0) / 2097152.0
 C_LO = LN_ALPHA - C_HI
 FLOPS = 2 * 2 * BH * S * S * D
 
-LA = 3
+LA = 4
 XMODE = "g"
 PIN = True
 PEMASK = tuple(range(2, 62, 5))
@@ -124,15 +124,19 @@ def tile_dotproductattention_t_kernel(tc, q, k, v, attn_mask, out):
                 )
             hd[h]["kTb"] = kT[:].bitcast(BF16).rearrange("w (j e) -> w j e", e=2)
 
-        def rgv(h):
+        def rgv(h, g):
             if h < 0 or h >= BH:
                 return
-            vg = wk.tile([P, D * NT], BF16, tag="vg", name="vg", align_bytes=64, bufs=2)
-            nc.vector.tensor_copy(
-                out=vg[:].rearrange("p (c i t) -> p c t i", i=4, t=NT),
-                in_=hd[h]["v"][:].rearrange("p (t c i) -> p c t i", t=NT, i=4),
+            if g == 0:
+                vg_new = wk.tile([P, D * NT], BF16, tag="vg", name="vg", align_bytes=64, bufs=2)
+                hd[h]["vg"] = vg_new
+            hw = D // 2
+            nc.scalar.copy(
+                out=hd[h]["vg"][:, g * hw * NT:(g + 1) * hw * NT].rearrange("p (c i t) -> p c t i", i=4, t=NT),
+                in_=hd[h]["v"][:].rearrange("p (t d) -> p t d", t=NT)[:, :, g * hw:(g + 1) * hw].rearrange(
+                    "p t (c i) -> p c t i", i=4
+                ),
             )
-            hd[h]["vg"] = vg
 
         def qv(h):
             if h < 0 or h >= BH:
@@ -206,12 +210,14 @@ def tile_dotproductattention_t_kernel(tc, q, k, v, attn_mask, out):
             n = kk // 2
             a = kk % 2
             if n not in pr:
-                rsum_new = wk.tile([P, 2], F32, tag="rsum", name="rsum", bufs=6)
-                pr[n] = {"rsum": rsum_new}
+                pr[n] = {}
+            if "rsum" not in hd[kk // NT]:
+                rsum_new = wk.tile([P, NT], F32, tag="rsum", name="rsum", bufs=4)
+                hd[kk // NT]["rsum"] = rsum_new
             e_sb = wk.tile([P, S], BF16, tag="e_sb", name="e_sb", bufs=4)
             nc.scalar.activation(
                 out=e_sb[:], in_=tl[kk]["s_src"][:], func=EXP, bias=tl[kk]["negm"][:], scale=1.0,
-                accum_out=pr[n]["rsum"][:, a:a + 1],
+                accum_out=hd[kk // NT]["rsum"][:, kk % NT:kk % NT + 1],
             )
             tl[kk]["e_sb"] = e_sb
 
@@ -219,9 +225,9 @@ def tile_dotproductattention_t_kernel(tc, q, k, v, attn_mask, out):
             if n < 0 or n >= NPAIRS:
                 return
             grp = wk.tile([P, 2 * P * NT], BF16, tag="grp", name="grp", align_bytes=64, bufs=1)
-            if XMODE == "g" and n < NPAIRS - TAILS:
-                etc = wk.tile([P, 2 * NT * P], BF16, tag="etc", name="etc", bufs=3)
-                nc.scalar.copy(out=etc[:], in_=pr[n]["eT_ps"][:].rearrange("p a c i -> p (a c i)"))
+            if n < NPAIRS - TAILS:
+                etc = wk.tile([P, 2 * NT * P], BF16, tag="etc", name="etc", bufs=2)
+                nc.vector.tensor_copy(out=etc[:], in_=pr[n]["eT_ps"][:].rearrange("p a c i -> p (a c i)"))
                 nc.gpsimd.tensor_scalar(
                     out=grp[:].rearrange("p (a i c) -> p a i c", a=2, c=NT),
                     in0=etc[:].rearrange("p (a c i) -> p a i c", a=2, c=NT),
@@ -240,11 +246,15 @@ def tile_dotproductattention_t_kernel(tc, q, k, v, attn_mask, out):
             ecod = wk.tile([P, 2 * P], U32, tag="ecod", name="ecod", align_bytes=64, bufs=3)
             escl = wk.tile([P, 2 * P], U8, tag="escl", name="escl", align_bytes=64, bufs=3)
             nc.vector.quantize_mx(out=ecod[:].bitcast(FP8X4), scales=escl[:], in_=pr[n]["grp"][:])
-            rinv = wk.tile([P, 2], F32, tag="rinv", name="rinv", bufs=4)
-            nc.vector.reciprocal(rinv[:], pr[n]["rsum"][:])
             pr[n]["ecod"] = ecod
             pr[n]["escl"] = escl
-            pr[n]["rinv"] = rinv
+
+        def recip(h):
+            if h < 0 or h >= BH:
+                return
+            rinv = wk.tile([P, NT], F32, tag="rinv", name="rinv", bufs=3)
+            nc.vector.reciprocal(rinv[:], hd[h]["rsum"][:])
+            hd[h]["rinv"] = rinv
 
         def pv(n):
             if n < 0 or n >= NPAIRS:
@@ -274,15 +284,15 @@ def tile_dotproductattention_t_kernel(tc, q, k, v, attn_mask, out):
                 o_new = wk.tile([P, NT * D], F32, tag="o_sb", name="o_sb", bufs=3)
                 hd[h]["o_sb"] = o_new
             o_sb = hd[h]["o_sb"]
-            if n % 4 == 3:
+            if False:
                 nc.vector.tensor_scalar(
-                    out=o_sb[:, t * D:(t + 1) * D], in0=pr[n]["o_ps"][:, a, :], scalar1=pr[n]["rinv"][:, a:a + 1],
+                    out=o_sb[:, t * D:(t + 1) * D], in0=pr[n]["o_ps"][:, a, :], scalar1=hd[h]["rinv"][:, t:t + 1],
                     scalar2=None, op0=MULT,
                 )
             else:
                 nc.scalar.activation(
                     out=o_sb[:, t * D:(t + 1) * D], in_=pr[n]["o_ps"][:, a, :], func=COPY,
-                    scale=pr[n]["rinv"][:, a:a + 1],
+                    scale=hd[h]["rinv"][:, t:t + 1],
                 )
 
         def store(h):
@@ -323,25 +333,23 @@ def tile_dotproductattention_t_kernel(tc, q, k, v, attn_mask, out):
                 pv((s - 7) // 2)
             if s == -7:
                 xk(0)
+            badd(s + 1)
             if s + 1 in PEMASK:
-                badd(s + 1)
                 cmax(s + 1)
-            else:
-                badd(s + 1)
             if s not in PEMASK:
                 cmax(s)
-            if (s - 2) % 4 == 0:
-                rgv((s - 2) // 4)
             if (s - 4) % 4 == 0:
                 qv((s - 4) // 4)
             if (s - 6) % 2 == 0:
                 qe((s - 6) // 2)
+            if (s - 6) % 4 == 0:
+                recip((s - 6) // 4)
+            if (s - 4) % 2 == 0:
+                xe((s - 4) // 2)
             if s in PEMASK:
                 dexp(s)
             if s - 1 not in PEMASK:
                 dexp(s - 1)
-            if (s - 4) % 2 == 0:
-                xe((s - 4) // 2)
             if (s - 8) % 2 == 0:
                 oex(s - 8)
                 oex(s - 7)
@@ -349,3 +357,7 @@ def tile_dotproductattention_t_kernel(tc, q, k, v, attn_mask, out):
                 xq((s + 7) // 4)
             if (s + 5) % 4 == 0 and s > -5:
                 xk((s + 5) // 4)
+            if (s - 1) % 4 == 0:
+                rgv((s - 1) // 4, 0)
+            if (s - 3) % 4 == 0:
+                rgv((s - 3) // 4, 1)

@@ -30,10 +30,8 @@ C_LO = LN_ALPHA - C_HI
 FLOPS = 2 * 2 * BH * S * S * D
 
 LA = 4
-XMODE = "g"
-PIN = True
 PEMASK = tuple(range(2, 62, 5))
-TAILS = 1
+DECAY = True
 
 
 def tile_dotproductattention_t_kernel(tc, q, k, v, attn_mask, out):
@@ -46,8 +44,7 @@ def tile_dotproductattention_t_kernel(tc, q, k, v, attn_mask, out):
         ps_s = ctx.enter_context(tc.psum_pool(name="ps_s", bufs=4))
         ps_et = ctx.enter_context(tc.psum_pool(name="ps_et", bufs=2))
         ps_o = ctx.enter_context(tc.psum_pool(name="ps_o", bufs=1))
-        if PIN:
-            ctx.enter_context(tc.manual_schedule())
+        ctx.enter_context(tc.manual_schedule())
 
         ident32 = const.tile([P, P], F32)
         make_identity(nc, ident32[:])
@@ -73,8 +70,14 @@ def tile_dotproductattention_t_kernel(tc, q, k, v, attn_mask, out):
         pr = {}
         tl = {}
 
+        def head_ok(h):
+            return 0 <= h < BH
+
+        def tile_ok(kk):
+            return 0 <= kk < NTILES
+
         def load(h):
-            if h < 0 or h >= BH:
+            if not head_ok(h):
                 return
             q_sb = ld.tile([P, NT * D], BF16, tag="q", name="q_sb")
             nc.sync.dma_start(out=q_sb[:], in_=q[h].rearrange("(p t) d -> p (t d)", t=NT))
@@ -90,7 +93,7 @@ def tile_dotproductattention_t_kernel(tc, q, k, v, attn_mask, out):
             hd[h] = {"q": q_sb, "k": k_sb, "m": m_sb, "v": v_sb}
 
         def tqk(h, which):
-            if h < 0 or h >= BH:
+            if not head_ok(h):
                 return
             src = hd[h][which][:].bitcast(F32)
             if h == 0 and which == "k":
@@ -102,44 +105,37 @@ def tile_dotproductattention_t_kernel(tc, q, k, v, attn_mask, out):
             hd[h][which + "ps"] = t_ps
 
         def xq(h):
-            if h < 0 or h >= BH:
+            if not head_ok(h):
                 return
             qT = wk.tile([P, S], F32, tag="qT", name="qT", bufs=2)
             nc.scalar.copy(out=qT[:], in_=hd[h]["qps"][:])
             hd[h]["qTb"] = qT[:].bitcast(BF16).rearrange("w (t p e) -> w t p e", t=NT, e=2)
 
         def xk(h):
-            if h < 0 or h >= BH:
+            if not head_ok(h):
                 return
             kT = wk.tile([P, S], F32, tag="kT", name="kT", bufs=2)
+            dst = kT[:].rearrange("w (p t) -> w p t", t=NT)
+            src = hd[h]["kps"][:].rearrange("w (t p) -> w p t", t=NT)
             if h == 0:
-                nc.vector.tensor_copy(
-                    out=kT[:].rearrange("w (p t) -> w p t", t=NT),
-                    in_=hd[h]["kps"][:].rearrange("w (t p) -> w p t", t=NT),
-                )
+                nc.vector.tensor_copy(out=dst, in_=src)
             else:
-                nc.scalar.copy(
-                    out=kT[:].rearrange("w (p t) -> w p t", t=NT),
-                    in_=hd[h]["kps"][:].rearrange("w (t p) -> w p t", t=NT),
-                )
+                nc.scalar.copy(out=dst, in_=src)
             hd[h]["kTb"] = kT[:].bitcast(BF16).rearrange("w (j e) -> w j e", e=2)
 
-        def rgv(h, g):
-            if h < 0 or h >= BH:
+        def rgv(h):
+            if not head_ok(h):
                 return
-            if g == 0:
-                vg_new = wk.tile([P, D * NT], BF16, tag="vg", name="vg", align_bytes=64, bufs=2)
-                hd[h]["vg"] = vg_new
-            hw = D // 2
-            nc.scalar.copy(
-                out=hd[h]["vg"][:, g * hw * NT:(g + 1) * hw * NT].rearrange("p (c i t) -> p c t i", i=4, t=NT),
-                in_=hd[h]["v"][:].rearrange("p (t d) -> p t d", t=NT)[:, :, g * hw:(g + 1) * hw].rearrange(
-                    "p t (c i) -> p c t i", i=4
-                ),
+            vg = wk.tile([P, D * NT], BF16, tag="vg", name="vg", align_bytes=64, bufs=1)
+            nc.gpsimd.tensor_scalar(
+                out=vg[:].rearrange("p (d t) -> p d t", t=NT),
+                in0=hd[h]["v"][:].rearrange("p (t d) -> p d t", t=NT),
+                scalar1=1.0, scalar2=0.0, op0=MULT, op1=ADD,
             )
+            hd[h]["vg"] = vg
 
         def qv(h):
-            if h < 0 or h >= BH:
+            if not head_ok(h):
                 return
             vcod = wk.tile([P, D], U32, tag="vcod", name="vcod", align_bytes=64, bufs=3)
             vscl = wk.tile([P, D], U8, tag="vscl", name="vscl", align_bytes=64, bufs=3)
@@ -148,7 +144,7 @@ def tile_dotproductattention_t_kernel(tc, q, k, v, attn_mask, out):
             hd[h]["vscl"] = vscl
 
         def mm(kq, e):
-            if kq < 0 or kq >= NTILES:
+            if not tile_ok(kq):
                 return
             st = hd[kq // NT]
             t = kq % NT
@@ -156,12 +152,18 @@ def tile_dotproductattention_t_kernel(tc, q, k, v, attn_mask, out):
                 s_new = ps_s.tile([P, S], F32, tag="s", name="s_ps")
                 tl[kq] = {"s_ps": s_new}
             s_ps = tl[kq]["s_ps"]
-            nc.tensor.matmul(s_ps[:], lhsT=st["qTb"][:, t, :, e], rhs=st["kTb"][:, :, e], start=(e == 0), stop=False)
-            if e == 1 and kq in PEMASK:
-                nc.tensor.matmul(s_ps[:], lhsT=identb[:], rhs=st["m"][:, t * S:(t + 1) * S], start=False, stop=False)
+            masked = kq in PEMASK
+            nc.tensor.matmul(
+                s_ps[:], lhsT=st["qTb"][:, t, :, e], rhs=st["kTb"][:, :, e], start=(e == 0),
+                stop=(e == 1 and not masked and not DECAY),
+            )
+            if e == 1 and masked:
+                nc.tensor.matmul(
+                    s_ps[:], lhsT=identb[:], rhs=st["m"][:, t * S:(t + 1) * S], start=False, stop=(not DECAY)
+                )
 
         def dec(kq, cs):
-            if kq < 0 or kq >= NTILES:
+            if not tile_ok(kq) or not DECAY:
                 return
             s_ps = tl[kq]["s_ps"]
             for c in cs:
@@ -175,18 +177,18 @@ def tile_dotproductattention_t_kernel(tc, q, k, v, attn_mask, out):
                 )
 
         def etr(ke, cs):
-            if ke < 0 or ke >= NTILES:
+            if not tile_ok(ke):
                 return
             n = ke // 2
             a = ke % 2
             if a == 0 and cs[0] == 0:
                 eT_new = ps_et.tile([P, 2, NT, P], BF16, tag="et", name="eT_ps")
-                pr[n]["eT_ps"] = eT_new
+                pr[n] = {"eT_ps": eT_new}
             for c in cs:
                 nc.tensor.transpose(pr[n]["eT_ps"][:, a, c, :], tl[ke]["e_sb"][:, c * P:(c + 1) * P], identb[:])
 
         def badd(kk):
-            if kk < 0 or kk >= NTILES:
+            if not tile_ok(kk):
                 return
             st = hd[kk // NT]
             t = kk % NT
@@ -198,59 +200,66 @@ def tile_dotproductattention_t_kernel(tc, q, k, v, attn_mask, out):
                 tl[kk]["s_src"] = s_sb
 
         def cmax(kk):
-            if kk < 0 or kk >= NTILES:
+            if not tile_ok(kk):
                 return
             negm = wk.tile([P, 1], F32, tag="negm", name="negm", bufs=4)
             nc.vector.tensor_reduce(out=negm[:], in_=tl[kk]["s_src"][:], axis=AX_X, op=MAX, negate=True)
             tl[kk]["negm"] = negm
 
         def dexp(kk):
-            if kk < 0 or kk >= NTILES:
+            if not tile_ok(kk):
                 return
-            n = kk // 2
-            a = kk % 2
-            if n not in pr:
-                pr[n] = {}
-            if "rsum" not in hd[kk // NT]:
+            st = hd[kk // NT]
+            t = kk % NT
+            if "rsum" not in st:
                 rsum_new = wk.tile([P, NT], F32, tag="rsum", name="rsum", bufs=4)
-                hd[kk // NT]["rsum"] = rsum_new
-            e_sb = wk.tile([P, S], BF16, tag="e_sb", name="e_sb", bufs=4)
+                st["rsum"] = rsum_new
+            e_sb = wk.tile([P, S], BF16, tag="e_sb", name="e_sb", bufs=5)
             nc.scalar.activation(
                 out=e_sb[:], in_=tl[kk]["s_src"][:], func=EXP, bias=tl[kk]["negm"][:], scale=1.0,
-                accum_out=hd[kk // NT]["rsum"][:, kk % NT:kk % NT + 1],
+                accum_out=st["rsum"][:, t:t + 1],
             )
             tl[kk]["e_sb"] = e_sb
 
-        def xe(n):
-            if n < 0 or n >= NPAIRS:
+        def xv(h):
+            if not head_ok(h):
                 return
-            grp = wk.tile([P, 2 * P * NT], BF16, tag="grp", name="grp", align_bytes=64, bufs=1)
-            if n < NPAIRS - TAILS:
-                etc = wk.tile([P, 2 * NT * P], BF16, tag="etc", name="etc", bufs=2)
-                nc.vector.tensor_copy(out=etc[:], in_=pr[n]["eT_ps"][:].rearrange("p a c i -> p (a c i)"))
-                nc.gpsimd.tensor_scalar(
-                    out=grp[:].rearrange("p (a i c) -> p a i c", a=2, c=NT),
-                    in0=etc[:].rearrange("p (a c i) -> p a i c", a=2, c=NT),
-                    scalar1=1.0, scalar2=0.0, op0=MULT, op1=ADD,
-                )
-            else:
-                nc.scalar.copy(
-                    out=grp[:].rearrange("p (a i c) -> p a i c", a=2, c=NT),
-                    in_=pr[n]["eT_ps"][:].rearrange("p a c i -> p a i c"),
-                )
-            pr[n]["grp"] = grp
+            n = 2 * h
+            etc = wk.tile([P, 2 * NT * P], BF16, tag="etc", name="etc", bufs=2)
+            nc.vector.tensor_copy(out=etc[:], in_=pr[n]["eT_ps"][:].rearrange("p a c i -> p (a c i)"))
+            hd[h]["etc"] = etc
 
-        def qe(n):
-            if n < 0 or n >= NPAIRS:
+        def rge(h):
+            if not head_ok(h):
                 return
-            ecod = wk.tile([P, 2 * P], U32, tag="ecod", name="ecod", align_bytes=64, bufs=3)
-            escl = wk.tile([P, 2 * P], U8, tag="escl", name="escl", align_bytes=64, bufs=3)
-            nc.vector.quantize_mx(out=ecod[:].bitcast(FP8X4), scales=escl[:], in_=pr[n]["grp"][:])
-            pr[n]["ecod"] = ecod
-            pr[n]["escl"] = escl
+            grp = wk.tile([P, NT * P * NT], BF16, tag="grp", name="grp", align_bytes=64, bufs=1)
+            nc.gpsimd.tensor_scalar(
+                out=grp[:, 0:2 * P * NT].rearrange("p (a i c) -> p a i c", a=2, c=NT),
+                in0=hd[h]["etc"][:].rearrange("p (a c i) -> p a i c", a=2, c=NT),
+                scalar1=1.0, scalar2=0.0, op0=MULT, op1=ADD,
+            )
+            hd[h]["grp"] = grp
+
+        def xs(h):
+            if not head_ok(h):
+                return
+            n = 2 * h + 1
+            nc.scalar.copy(
+                out=hd[h]["grp"][:, 2 * P * NT:4 * P * NT].rearrange("p (a i c) -> p a i c", a=2, c=NT),
+                in_=pr[n]["eT_ps"][:].rearrange("p a c i -> p a i c"),
+            )
+
+        def qe(h):
+            if not head_ok(h):
+                return
+            ecod = wk.tile([P, NT * P], U32, tag="ecod", name="ecod", align_bytes=64, bufs=2)
+            escl = wk.tile([P, NT * P], U8, tag="escl", name="escl", align_bytes=64, bufs=2)
+            nc.vector.quantize_mx(out=ecod[:].bitcast(FP8X4), scales=escl[:], in_=hd[h]["grp"][:])
+            hd[h]["ecod"] = ecod
+            hd[h]["escl"] = escl
 
         def recip(h):
-            if h < 0 or h >= BH:
+            if not head_ok(h):
                 return
             rinv = wk.tile([P, NT], F32, tag="rinv", name="rinv", bufs=3)
             nc.vector.reciprocal(rinv[:], hd[h]["rsum"][:])
@@ -262,10 +271,11 @@ def tile_dotproductattention_t_kernel(tc, q, k, v, attn_mask, out):
             st = hd[n // 2]
             o_ps = ps_o.tile([P, 2, D], F32, tag="o", name="o_ps")
             for a in range(2):
+                t = 2 * (n % 2) + a
                 nc.tensor.matmul_mx(
                     out=o_ps[:, a, :],
-                    lhsT=pr[n]["ecod"][:, a * P:(a + 1) * P].bitcast(FP8X4),
-                    lhsT_scale=pr[n]["escl"][:, a * P:(a + 1) * P],
+                    lhsT=st["ecod"][:, t * P:(t + 1) * P].bitcast(FP8X4),
+                    lhsT_scale=st["escl"][:, t * P:(t + 1) * P],
                     rhs=st["vcod"][:].bitcast(FP8X4),
                     rhs_scale=st["vscl"][:],
                     start=True,
@@ -273,64 +283,56 @@ def tile_dotproductattention_t_kernel(tc, q, k, v, attn_mask, out):
                 )
             pr[n]["o_ps"] = o_ps
 
-        def oex(kk):
-            if kk < 0 or kk >= NTILES:
+        def oex(n):
+            if n < 0 or n >= NPAIRS:
                 return
-            h = kk // NT
-            t = kk % NT
-            n = kk // 2
-            a = kk % 2
-            if t == 0:
+            h = n // 2
+            if n % 2 == 0:
                 o_new = wk.tile([P, NT * D], F32, tag="o_sb", name="o_sb", bufs=3)
                 hd[h]["o_sb"] = o_new
-            o_sb = hd[h]["o_sb"]
-            if False:
-                nc.vector.tensor_scalar(
-                    out=o_sb[:, t * D:(t + 1) * D], in0=pr[n]["o_ps"][:, a, :], scalar1=hd[h]["rinv"][:, t:t + 1],
-                    scalar2=None, op0=MULT,
-                )
-            else:
+            for a in range(2):
+                t = 2 * (n % 2) + a
                 nc.scalar.activation(
-                    out=o_sb[:, t * D:(t + 1) * D], in_=pr[n]["o_ps"][:, a, :], func=COPY,
+                    out=hd[h]["o_sb"][:, t * D:(t + 1) * D], in_=pr[n]["o_ps"][:, a, :], func=COPY,
                     scale=hd[h]["rinv"][:, t:t + 1],
                 )
 
-        def store(h):
-            if h < 0 or h >= BH:
+        def store(h, lo, hi):
+            if not head_ok(h):
                 return
-            nc.sync.dma_start(out=out[h].rearrange("(p t) d -> p (t d)", t=NT), in_=hd[h]["o_sb"][:])
-
-        def store_half(h, half):
             nc.sync.dma_start(
-                out=out[h].rearrange("(p t) d -> p (t d)", t=NT)[:, half * 2 * D:(half + 1) * 2 * D],
-                in_=hd[h]["o_sb"][:, half * 2 * D:(half + 1) * 2 * D],
+                out=out[h].rearrange("(p t) d -> p (t d)", t=NT)[:, lo * D:hi * D], in_=hd[h]["o_sb"][:, lo * D:hi * D]
             )
 
         for h in range(LA):
             load(h)
         for s in range(-8, NTILES + 13):
-            if s >= 0 and s % 4 == 0:
-                load(s // 4 + LA)
-            if (s - 11) % 4 == 0 and (s - 11) // 4 < BH - 1:
-                store((s - 11) // 4)
-            if s == NTILES + 5:
-                store_half(BH - 1, 0)
-            if s == NTILES + 7:
-                store_half(BH - 1, 1)
+            r = s % 4
+            g = s // 4
+            if s >= 0 and r == 0:
+                load(g + LA)
+                if g - 3 < BH - 1:
+                    store(g - 3, 0, NT)
+            if s == NTILES + 6:
+                store(BH - 1, 0, 2)
+            if s == NTILES + 8:
+                store(BH - 1, 2, NT)
             mm(s + 3, 0)
             dec(s + 2, (0, 1))
             etr(s - 2, (0, 1))
             mm(s + 3, 1)
             dec(s + 2, (2, 3))
             etr(s - 2, (2, 3))
-            if (s + 8) % 4 == 0:
-                tqk((s + 8) // 4, "q")
-            if s == -8:
-                tqk(0, "k")
-            if (s + 6) % 4 == 0 and s > -6:
-                tqk((s + 6) // 4, "k")
-            if (s - 7) % 2 == 0:
-                pv((s - 7) // 2)
+            if r == 0:
+                tqk(g + 2, "q")
+                if s == -8:
+                    tqk(0, "k")
+            if r == 2 and s > -6:
+                tqk(g + 2, "k")
+            if r == 0:
+                pv(2 * (g - 2))
+            if r == 2:
+                pv(2 * (g - 2) + 1)
             if s == -7:
                 xk(0)
             badd(s + 1)
@@ -338,26 +340,25 @@ def tile_dotproductattention_t_kernel(tc, q, k, v, attn_mask, out):
                 cmax(s + 1)
             if s not in PEMASK:
                 cmax(s)
-            if (s - 4) % 4 == 0:
-                qv((s - 4) // 4)
-            if (s - 6) % 2 == 0:
-                qe((s - 6) // 2)
-            if (s - 6) % 4 == 0:
-                recip((s - 6) // 4)
-            if (s - 4) % 2 == 0:
-                xe((s - 4) // 2)
+            if r == 0:
+                xv(g - 1)
+            if r == 3:
+                qe(g - 1)
+                qv(g)
+                recip(g - 1)
+            if r == 0:
+                rgv(g)
+                rge(g - 1)
             if s in PEMASK:
                 dexp(s)
             if s - 1 not in PEMASK:
                 dexp(s - 1)
-            if (s - 8) % 2 == 0:
-                oex(s - 8)
-                oex(s - 7)
-            if (s + 7) % 4 == 0:
-                xq((s + 7) // 4)
-            if (s + 5) % 4 == 0 and s > -5:
-                xk((s + 5) // 4)
-            if (s - 1) % 4 == 0:
-                rgv((s - 1) // 4, 0)
-            if (s - 3) % 4 == 0:
-                rgv((s - 3) // 4, 1)
+            if r == 1:
+                xq(g + 2)
+                oex(2 * (g - 2))
+            if r == 2:
+                xs(g - 1)
+            if r == 3:
+                if s > -5:
+                    xk(g + 2)
+                oex(2 * (g - 2) + 1)

@@ -318,9 +318,18 @@ def tile_dotproductattention_t_kernel(tc, q, k, v, attn_mask, out):
             if s == NTILES + 8:
                 store(BH - 1, 2, NT)
             mm(s + 3, 0)
-            dec(s + 2, (0, 1))
-            etr(s - 2, (0, 1))
-            mm(s + 3, 1)
+            if r == 1:
+                pv(2 * (g - 2))
+            if r == 3:
+                pv(2 * (g - 2) + 1)
+            if r == 1 or r == 3:
+                mm(s + 3, 1)
+                dec(s + 2, (0, 1))
+                etr(s - 2, (0, 1))
+            else:
+                dec(s + 2, (0, 1))
+                etr(s - 2, (0, 1))
+                mm(s + 3, 1)
             dec(s + 2, (2, 3))
             etr(s - 2, (2, 3))
             if r == 0:
@@ -329,10 +338,6 @@ def tile_dotproductattention_t_kernel(tc, q, k, v, attn_mask, out):
                     tqk(0, "k")
             if r == 2 and s > -6:
                 tqk(g + 2, "k")
-            if r == 0:
-                pv(2 * (g - 2))
-            if r == 2:
-                pv(2 * (g - 2) + 1)
             if s == -7:
                 xk(0)
             badd(s + 1)

import math
from contextlib import ExitStack

import concourse.mybir as mybir
from concourse.masks import make_identity

F32 = mybir.dt.float32
BF16 = mybir.dt.bfloat16
I32 = mybir.dt.int32
U32 = mybir.dt.uint32
U8 = mybir.dt.uint8
FP8X4 = mybir.dt.float8_e4m3fn_x4
ADD = mybir.AluOpType.add
MULT = mybir.AluOpType.mult
MAX = mybir.AluOpType.max
EXP = mybir.ActivationFunctionType.Exp
COPY = mybir.ActivationFunctionType.Copy
AX_X = mybir.AxisListType.X

P = 128
BH, S, D = 16, 512, 256
NT = S // P
NTILES = BH * NT
NPAIRS = NTILES // 2
ALPHA = 0.99
EPS = 1e-10
LN_ALPHA = math.log(ALPHA)
C_HI = round(LN_ALPHA * 2097152.0) / 2097152.0
C_LO = LN_ALPHA - C_HI
FLOPS = 2 * 2 * BH * S * S * D

LA = 4
PEMASK = tuple(range(2, 62, 5))
DECAY = True


def tile_dotproductattention_t_kernel(tc, q, k, v, attn_mask, out):
    nc = tc.nc
    with ExitStack() as ctx:
        const = ctx.enter_context(tc.tile_pool(name="const", bufs=1))
        ld = ctx.enter_context(tc.tile_pool(name="ld", bufs=LA + 1))
        wk = ctx.enter_context(tc.tile_pool(name="wk", bufs=2))
        ps_tr = ctx.enter_context(tc.psum_pool(name="ps_tr", bufs=1))
        ps_s = ctx.enter_context(tc.psum_pool(name="ps_s", bufs=4))
        ps_et = ctx.enter_context(tc.psum_pool(name="ps_et", bufs=2))
        ps_o = ctx.enter_context(tc.psum_pool(name="ps_o", bufs=1))
        ctx.enter_context(tc.manual_schedule())

        ident32 = const.tile([P, P], F32)
        make_identity(nc, ident32[:])
        identb = const.tile([P, P], BF16)
        make_identity(nc, identb[:])

        j_i = const.tile([P, NT], I32)
        nc.gpsimd.iota(j_i[:], pattern=[[P, NT]], base=0, channel_multiplier=1)
        j_f = const.tile([P, NT], F32)
        nc.vector.tensor_copy(out=j_f[:], in_=j_i[:])
        n_f = const.tile([P, NT], F32)
        nc.vector.tensor_scalar(out=n_f[:], in0=j_f[:], scalar1=-1.0, scalar2=float(S - 1), op0=MULT, op1=ADD)
        grow = const.tile([P, NT], F32)
        nc.scalar.activation(out=grow[:], in_=n_f[:], func=EXP, scale=-LN_ALPHA)
        low = const.tile([P, NT], F32)
        nc.vector.tensor_scalar(out=low[:], in0=n_f[:], scalar1=C_LO, scalar2=None, op0=MULT)
        low2 = const.tile([P, NT], F32)
        nc.vector.scalar_tensor_tensor(out=low2[:], in0=grow[:], scalar=EPS, in1=low[:], op0=MULT, op1=ADD)
        dcol = const.tile([P, NT], F32)
        nc.vector.scalar_tensor_tensor(out=dcol[:], in0=n_f[:], scalar=C_HI, in1=low2[:], op0=MULT, op1=ADD)

        hd = {}
        pr = {}
        tl = {}

        def head_ok(h):
            return 0 <= h < BH

        def tile_ok(kk):
            return 0 <= kk < NTILES

        def load(h):
            if not head_ok(h):
                return
            q_sb = ld.tile([P, NT * D], BF16, tag="q", name="q_sb")
            nc.sync.dma_start(out=q_sb[:], in_=q[h].rearrange("(p t) d -> p (t d)", t=NT))
            k_sb = ld.tile([P, NT * D], BF16, tag="k", name="k_sb")
            nc.sync.dma_start(out=k_sb[:], in_=k[h].rearrange("(p t) d -> p (t d)", t=NT))
            m_sb = ld.tile([P, NT * S], BF16, tag="m", name="m_sb")
            nc.sync.dma_start(out=m_sb[:], in_=attn_mask[h].rearrange("(p t) j -> p (t j)", t=NT))
            v_sb = ld.tile([P, NT * D], BF16, tag="v", name="v_sb")
            nc.sync.dma_start(
                out=v_sb[:].rearrange("p (t d) -> p t d", t=NT),
                in_=v[h].rearrange("(t p) d -> p t d", p=P),
            )
            hd[h] = {"q": q_sb, "k": k_sb, "m": m_sb, "v": v_sb}

        def tqk(h, which):
            if not head_ok(h):
                return
            src = hd[h][which][:].bitcast(F32)
            if h == 0 and which == "k":
                t_ps = ps_o.tile([P, S], F32, tag="o", name="t_ps0")
            else:
                t_ps = ps_tr.tile([P, S], F32, tag="tr", name="t_ps")
            for t in range(NT):
                nc.tensor.transpose(t_ps[:, t * P:(t + 1) * P], src[:, t * P:(t + 1) * P], ident32[:])
            hd[h][which + "ps"] = t_ps

        def xq(h):
            if not head_ok(h):
                return
            qT = wk.tile([P, S], F32, tag="qT", name="qT", bufs=2)
            nc.scalar.copy(out=qT[:], in_=hd[h]["qps"][:])
            hd[h]["qTb"] = qT[:].bitcast(BF16).rearrange("w (t p e) -> w t p e", t=NT, e=2)

        def xk(h):
            if not head_ok(h):
                return
            kT = wk.tile([P, S], F32, tag="kT", name="kT", bufs=2)
            dst = kT[:].rearrange("w (p t) -> w p t", t=NT)
            src = hd[h]["kps"][:].rearrange("w (t p) -> w p t", t=NT)
            if h == 0:
                nc.vector.tensor_copy(out=dst, in_=src)
            else:
                nc.scalar.copy(out=dst, in_=src)
            hd[h]["kTb"] = kT[:].bitcast(BF16).rearrange("w (j e) -> w j e", e=2)

        def rgv(h):
            if not head_ok(h):
                return
            vg = wk.tile([P, D * NT], BF16, tag="vg", name="vg", align_bytes=64, bufs=1)
            nc.gpsimd.tensor_scalar(
                out=vg[:].rearrange("p (d t) -> p d t", t=NT),
                in0=hd[h]["v"][:].rearrange("p (t d) -> p d t", t=NT),
                scalar1=1.0, scalar2=0.0, op0=MULT, op1=ADD,
            )
            hd[h]["vg"] = vg

        def qv(h):
            if not head_ok(h):
                return
            vcod = wk.tile([P, D], U32, tag="vcod", name="vcod", align_bytes=64, bufs=3)
            vscl = wk.tile([P, D], U8, tag="vscl", name="vscl", align_bytes=64, bufs=3)
            nc.vector.quantize_mx(out=vcod[:].bitcast(FP8X4), scales=vscl[:], in_=hd[h]["vg"][:])
            hd[h]["vcod"] = vcod
            hd[h]["vscl"] = vscl

        def mm(kq, e):
            if not tile_ok(kq):
                return
            st = hd[kq // NT]
            t = kq % NT
            if e == 0:
                s_new = ps_s.tile([P, S], F32, tag="s", name="s_ps")
                tl[kq] = {"s_ps": s_new}
            s_ps = tl[kq]["s_ps"]
            masked = kq in PEMASK
            nc.tensor.matmul(
                s_ps[:], lhsT=st["qTb"][:, t, :, e], rhs=st["kTb"][:, :, e], start=(e == 0),
                stop=(e == 1 and not masked and not DECAY),
            )
            if e == 1 and masked:
                nc.tensor.matmul(
                    s_ps[:], lhsT=identb[:], rhs=st["m"][:, t * S:(t + 1) * S], start=False, stop=(not DECAY)
                )

        def dec(kq, cs):
            if not tile_ok(kq) or not DECAY:
                return
            s_ps = tl[kq]["s_ps"]
            for c in cs:
                nc.tensor.matmul(
                    s_ps[:, c * P:(c + 1) * P],
                    lhsT=dcol[:, c:c + 1].to_broadcast([P, P]),
                    rhs=ident32[:],
                    start=False,
                    stop=(c == NT - 1),
                    is_transpose=True,
                )

        def etr(ke, cs):
            if not tile_ok(ke):
                return
            n = ke // 2
            a = ke % 2
            if a == 0 and cs[0] == 0:
                eT_new = ps_et.tile([P, 2, NT, P], BF16, tag="et", name="eT_ps")
                pr[n] = {"eT_ps": eT_new}
            for c in cs:
                nc.tensor.transpose(pr[n]["eT_ps"][:, a, c, :], tl[ke]["e_sb"][:, c * P:(c + 1) * P], identb[:])

        def badd(kk):
            if not tile_ok(kk):
                return
            st = hd[kk // NT]
            t = kk % NT
            if kk in PEMASK:
                tl[kk]["s_src"] = tl[kk]["s_ps"]
            else:
                s_sb = wk.tile([P, S], F32, tag="s_sb", name="s_sb", bufs=5)
                nc.vector.tensor_tensor(out=s_sb[:], in0=tl[kk]["s_ps"][:], in1=st["m"][:, t * S:(t + 1) * S], op=ADD)
                tl[kk]["s_src"] = s_sb

        def cmax(kk):
            if not tile_ok(kk):
                return
            negm = wk.tile([P, 1], F32, tag="negm", name="negm", bufs=4)
            nc.vector.tensor_reduce(out=negm[:], in_=tl[kk]["s_src"][:], axis=AX_X, op=MAX, negate=True)
            tl[kk]["negm"] = negm

        def dexp(kk):
            if not tile_ok(kk):
                return
            st = hd[kk // NT]
            t = kk % NT
            if "rsum" not in st:
                rsum_new = wk.tile([P, NT], F32, tag="rsum", name="rsum", bufs=4)
                st["rsum"] = rsum_new
            e_sb = wk.tile([P, S], BF16, tag="e_sb", name="e_sb", bufs=5)
            nc.scalar.activation(
                out=e_sb[:], in_=tl[kk]["s_src"][:], func=EXP, bias=tl[kk]["negm"][:], scale=1.0,
                accum_out=st["rsum"][:, t:t + 1],
            )
            tl[kk]["e_sb"] = e_sb

        def xv(h):
            if not head_ok(h):
                return
            n = 2 * h
            etc = wk.tile([P, 2 * NT * P], BF16, tag="etc", name="etc", bufs=2)
            nc.vector.tensor_copy(out=etc[:], in_=pr[n]["eT_ps"][:].rearrange("p a c i -> p (a c i)"))
            hd[h]["etc"] = etc

        def rge(h):
            if not head_ok(h):
                return
            grp = wk.tile([P, NT * P * NT], BF16, tag="grp", name="grp", align_bytes=64, bufs=1)
            nc.gpsimd.tensor_scalar(
                out=grp[:, 0:2 * P * NT].rearrange("p (a i c) -> p a i c", a=2, c=NT),
                in0=hd[h]["etc"][:].rearrange("p (a c i) -> p a i c", a=2, c=NT),
                scalar1=1.0, scalar2=0.0, op0=MULT, op1=ADD,
            )
            hd[h]["grp"] = grp

        def xs(h):
            if not head_ok(h):
                return
            n = 2 * h + 1
            nc.scalar.copy(
                out=hd[h]["grp"][:, 2 * P * NT:4 * P * NT].rearrange("p (a i c) -> p a i c", a=2, c=NT),
                in_=pr[n]["eT_ps"][:].rearrange("p a c i -> p a i c"),
            )

        def qe(h):
            if not head_ok(h):
                return
            ecod = wk.tile([P, NT * P], U32, tag="ecod", name="ecod", align_bytes=64, bufs=2)
            escl = wk.tile([P, NT * P], U8, tag="escl", name="escl", align_bytes=64, bufs=2)
            nc.vector.quantize_mx(out=ecod[:].bitcast(FP8X4), scales=escl[:], in_=hd[h]["grp"][:])
            hd[h]["ecod"] = ecod
            hd[h]["escl"] = escl

        def recip(h):
            if not head_ok(h):
                return
            rinv = wk.tile([P, NT], F32, tag="rinv", name="rinv", bufs=3)
            nc.vector.reciprocal(rinv[:], hd[h]["rsum"][:])
            hd[h]["rinv"] = rinv

        def pv(n):
            if n < 0 or n >= NPAIRS:
                return
            st = hd[n // 2]
            o_ps = ps_o.tile([P, 2, D], F32, tag="o", name="o_ps")
            for a in range(2):
                t = 2 * (n % 2) + a
                nc.tensor.matmul_mx(
                    out=o_ps[:, a, :],
                    lhsT=st["ecod"][:, t * P:(t + 1) * P].bitcast(FP8X4),
                    lhsT_scale=st["escl"][:, t * P:(t + 1) * P],
                    rhs=st["vcod"][:].bitcast(FP8X4),
                    rhs_scale=st["vscl"][:],
                    start=True,
                    stop=True,
                )
            pr[n]["o_ps"] = o_ps

        def oex(n):
            if n < 0 or n >= NPAIRS:
                return
            h = n // 2
            if n % 2 == 0:
                o_new = wk.tile([P, NT * D], F32, tag="o_sb", name="o_sb", bufs=3)
                hd[h]["o_sb"] = o_new
            for a in range(2):
                t = 2 * (n % 2) + a
                nc.scalar.activation(
                    out=hd[h]["o_sb"][:, t * D:(t + 1) * D], in_=pr[n]["o_ps"][:, a, :], func=COPY,
                    scale=hd[h]["rinv"][:, t:t + 1],
                )

        def store(h, lo, hi):
            if not head_ok(h):
                return
            nc.sync.dma_start(
                out=out[h].rearrange("(p t) d -> p (t d)", t=NT)[:, lo * D:hi * D], in_=hd[h]["o_sb"][:, lo * D:hi * D]
            )

        for h in range(LA):
            load(h)
        for s in range(-8, NTILES + 13):
            r = s % 4
            g = s // 4
            if s >= 0 and r == 0:
                load(g + LA)
                if g - 3 < BH - 1:
                    store(g - 3, 0, NT)
            if s == NTILES + 6:
                store(BH - 1, 0, 2)
            if s == NTILES + 8:
                store(BH - 1, 2, NT)
            mm(s + 3, 0)
            if r == 1:
                pv(2 * (g - 2))
            if r == 3:
                pv(2 * (g - 2) + 1)
            if r == 1 or r == 3:
                mm(s + 3, 1)
                dec(s + 2, (0, 1))
                etr(s - 2, (0, 1))
            else:
                dec(s + 2, (0, 1))
                etr(s - 2, (0, 1))
                mm(s + 3, 1)
            dec(s + 2, (2, 3))
            etr(s - 2, (2, 3))
            if r == 0:
                tqk(g + 2, "q")
                if s == -8:
                    tqk(0, "k")
            if r == 2 and s > -6:
                tqk(g + 2, "k")
            if s == -7:
                xk(0)
            badd(s + 1)
            if s + 1 in PEMASK:
                cmax(s + 1)
            if s not in PEMASK:
                cmax(s)
            if r == 0:
                xv(g - 1)
            if r == 3:
                qe(g - 1)
                qv(g)
                recip(g - 1)
            if r == 0:
                rgv(g)
                rge(g - 1)
            if s in PEMASK:
                dexp(s)
            if s - 1 not in PEMASK:
                dexp(s - 1)
            if r == 1:
                xq(g + 2)
                oex(2 * (g - 2))
            if r == 2:
                xs(g - 1)
            if r == 3:
                if s > -5:
                    xk(g + 2)
                oex(2 * (g - 2) + 1)
